import numpy as np
import ml_dtypes

BF16 = ml_dtypes.bfloat16


def bf(x):
    return np.asarray(x, np.float32).astype(BF16)


def f32(x):
    return np.asarray(x, np.float32)


def f64(x):
    return np.asarray(x).astype(np.float64)


def striped(idx):
    return np.tile(idx.reshape(-1, 16).T, (8, 1))


C, S, B, Q, N = 128, 4096, 128, 20, 2560


def position_encoding():
    t = np.arange(1, Q + 1, dtype=np.float64)[None, :]
    k = np.arange(1, C + 1, dtype=np.float64)[:, None]
    return 1.0 - t / Q - (k / C) * (1.0 - 2.0 * t / Q)


def setup_inputs():
    return {"x": f32(np.random.standard_normal((C, S))), "pe": f32(np.tile(position_encoding(), (1, B))), "mem": f32(np.random.standard_normal((C, 1))), "w": bf(np.random.standard_normal((C, S)) / np.sqrt(C)), "offs": striped(np.random.permutation(np.tile(np.arange(S), 2))[:N])}


def reference(x, pe, mem, w, offs):
    idx = offs[:16].T.reshape(-1)
    prod = f64(x)[:, idx] * f64(pe)
    u = prod.reshape(C, B, Q).sum(axis=2) + f64(mem)
    return f64(w).T @ u

@@ -1,0 +1,86 @@
+import concourse.mybir as mybir
+
+F32 = mybir.dt.float32
+BF16 = mybir.dt.bfloat16
+U16 = mybir.dt.uint16
+MULT = mybir.AluOpType.mult
+ADD = mybir.AluOpType.add
+COPY = mybir.ActivationFunctionType.Copy
+INNERMOST = mybir.AxisListType.X
+
+C = 128
+S = 4096
+B = 128
+Q = 20
+N = B * Q
+
+PIECES = 4
+PIECE = N // PIECES
+PIECE_QUESTIONS = B // PIECES
+
+BLOCK = 128
+BLOCKS_IN_BANK = 4
+BANKS = S // (BLOCK * BLOCKS_IN_BANK)
+
+FLOPS = 2 * C * S * B
+
+
+def tile_memn2n_ss_kernel(tc, x, pe, mem, w, offs, out):
+    nc = tc.nc
+    with (
+        tc.tile_pool(name="held", bufs=1) as held,
+        tc.tile_pool(name="staging", bufs=BANKS) as staging,
+        tc.psum_pool(name="banks", bufs=BANKS) as banks,
+    ):
+        offsets = held.tile([C, N // 16], U16, name="offsets")
+        nc.sync.dma_start(offsets[:], offs)
+        table = held.tile([C, S], F32, name="table")
+        nc.sync.dma_start(table[:, : S // 2], x[:, : S // 2])
+        nc.scalar.dma_start(table[:, S // 2 :], x[:, S // 2 :])
+        pe_pieces = []
+        for i in range(PIECES):
+            pe_piece = held.tile([C, PIECE], F32, name=f"pe_piece{i}")
+            queue = nc.sync if i % 2 == 0 else nc.scalar
+            queue.dma_start(pe_piece[:], pe[:, i * PIECE : (i + 1) * PIECE])
+            pe_pieces.append(pe_piece)
+        readout = held.tile([C, 1], F32, name="readout")
+        nc.sync.dma_start(readout[:], mem)
+        weights = held.tile([C, S], BF16, name="weights")
+        nc.scalar.dma_start(weights[:], w)
+
+        sums = held.tile([C, B], F32, name="sums")
+        for i in range(PIECES):
+            prod = held.tile([C, PIECE], F32, name=f"prod{i}")
+            piece_offsets = offsets[:, i * PIECE // 16 : (i + 1) * PIECE // 16]
+            nc.vector.tensor_tensor(prod[:], table[:].indirect(piece_offsets), pe_pieces[i][:], MULT)
+            nc.vector.tensor_reduce(
+                sums[:, i * PIECE_QUESTIONS : (i + 1) * PIECE_QUESTIONS],
+                prod[:].rearrange("c (b q) -> c b q", q=Q),
+                INNERMOST,
+                ADD,
+            )
+
+        state = held.tile([C, B], BF16, name="state")
+        nc.vector.tensor_scalar_add(state[:], sums[:], readout[:, 0:1])
+
+        out_blocks = out.rearrange("(k p) b -> p k b", p=BLOCK)
+        for g in range(BANKS):
+            bank = banks.tile([BLOCK, BLOCKS_IN_BANK * B], F32, name="bank")
+            for j in range(BLOCKS_IN_BANK):
+                k = g * BLOCKS_IN_BANK + j
+                nc.tensor.matmul(
+                    bank[:, j * B : (j + 1) * B],
+                    weights[:, k * BLOCK : (k + 1) * BLOCK],
+                    state[:],
+                    start=True,
+                    stop=True,
+                )
+            staged = staging.tile([BLOCK, BLOCKS_IN_BANK * B], F32, name="staged")
+            if g % 2 == 0:
+                nc.vector.tensor_copy(staged[:], bank[:])
+            else:
+                nc.scalar.activation(staged[:], bank[:], COPY)
+            nc.sync.dma_start(
+                out_blocks[:, g * BLOCKS_IN_BANK : (g + 1) * BLOCKS_IN_BANK, :],
+                staged[:].rearrange("p (k b) -> p k b", b=B),
+            )

@@ -19,6 +19,7 @@ PIECE = N // PIECES
 PIECE_QUESTIONS = B // PIECES
 
 BLOCK = 128
+BLOCKS = S // BLOCK
 BLOCKS_IN_BANK = 4
 BANKS = S // (BLOCK * BLOCKS_IN_BANK)
 
@@ -63,14 +64,15 @@ def tile_memn2n_ss_kernel(tc, x, pe, mem, w, offs, out):
         state = held.tile([C, B], BF16, name="state")
         nc.vector.tensor_scalar_add(state[:], sums[:], readout[:, 0:1])
 
-        out_blocks = out.rearrange("(k p) b -> p k b", p=BLOCK)
+        weight_blocks = weights[:].rearrange("c (p k) -> c k p", k=BLOCKS)
+        out_blocks = out.rearrange("(p k) b -> p k b", k=BLOCKS)
         for g in range(BANKS):
             bank = banks.tile([BLOCK, BLOCKS_IN_BANK * B], F32, name="bank")
             for j in range(BLOCKS_IN_BANK):
                 k = g * BLOCKS_IN_BANK + j
                 nc.tensor.matmul(
                     bank[:, j * B : (j + 1) * B],
-                    weights[:, k * BLOCK : (k + 1) * BLOCK],
+                    weight_blocks[:, k, :],
                     state[:],
                     start=True,
                     stop=True,

@@ -14,14 +14,15 @@ B = 128
 Q = 20
 N = B * Q
 
-PIECES = 4
-PIECE = N // PIECES
-PIECE_QUESTIONS = B // PIECES
+PIECE_STARTS = (0, 320, 640, 1280, N)
+PIECES = len(PIECE_STARTS) - 1
+
+SCALAR_QUESTIONS = 48
 
 BLOCK = 128
 BLOCKS = S // BLOCK
 BLOCKS_IN_BANK = 4
-BANKS = S // (BLOCK * BLOCKS_IN_BANK)
+BANKS = BLOCKS // BLOCKS_IN_BANK
 
 FLOPS = 2 * C * S * B
 
@@ -35,31 +36,37 @@ def tile_memn2n_ss_kernel(tc, x, pe, mem, w, offs, out):
     ):
         offsets = held.tile([C, N // 16], U16, name="offsets")
         nc.sync.dma_start(offsets[:], offs)
-        table = held.tile([C, S], F32, name="table")
-        nc.sync.dma_start(table[:, : S // 2], x[:, : S // 2])
-        nc.scalar.dma_start(table[:, S // 2 :], x[:, S // 2 :])
         pe_pieces = []
         for i in range(PIECES):
-            pe_piece = held.tile([C, PIECE], F32, name=f"pe_piece{i}")
-            queue = nc.sync if i % 2 == 0 else nc.scalar
-            queue.dma_start(pe_piece[:], pe[:, i * PIECE : (i + 1) * PIECE])
-            pe_pieces.append(pe_piece)
+            pe_pieces.append(held.tile([C, PIECE_STARTS[i + 1] - PIECE_STARTS[i]], F32, name=f"pe_piece{i}"))
+        nc.sync.dma_start(pe_pieces[0][:], pe[:, PIECE_STARTS[0] : PIECE_STARTS[1]])
+        table = held.tile([C, S], F32, name="table")
+        nc.sync.dma_start(table[:, : S // 2], x[:, : S // 2])
+        nc.sync.dma_start(table[:, S // 2 :], x[:, S // 2 :])
+        for i in range(1, PIECES):
+            nc.sync.dma_start(pe_pieces[i][:], pe[:, PIECE_STARTS[i] : PIECE_STARTS[i + 1]])
+        weights = held.tile([C, S], BF16, name="weights")
+        nc.sync.dma_start(weights[:], w)
         readout = held.tile([C, 1], F32, name="readout")
         nc.sync.dma_start(readout[:], mem)
-        weights = held.tile([C, S], BF16, name="weights")
-        nc.scalar.dma_start(weights[:], w)
+
+        prod = held.tile([C, N], F32, name="prod")
+        for i in range(PIECES):
+            first, end = PIECE_STARTS[i], PIECE_STARTS[i + 1]
+            nc.vector.tensor_tensor(
+                prod[:, first:end], table[:].indirect(offsets[:, first // 16 : end // 16]), pe_pieces[i][:], MULT
+            )
 
         sums = held.tile([C, B], F32, name="sums")
-        for i in range(PIECES):
-            prod = held.tile([C, PIECE], F32, name=f"prod{i}")
-            piece_offsets = offsets[:, i * PIECE // 16 : (i + 1) * PIECE // 16]
-            nc.vector.tensor_tensor(prod[:], table[:].indirect(piece_offsets), pe_pieces[i][:], MULT)
-            nc.vector.tensor_reduce(
-                sums[:, i * PIECE_QUESTIONS : (i + 1) * PIECE_QUESTIONS],
-                prod[:].rearrange("c (b q) -> c b q", q=Q),
-                INNERMOST,
-                ADD,
-            )
+        unused = held.tile([C, Q], F32, name="unused")
+        for b in range(SCALAR_QUESTIONS):
+            nc.scalar.activation(unused[:], prod[:, b * Q : (b + 1) * Q], COPY, accum_out=sums[:, b : b + 1])
+        nc.vector.tensor_reduce(
+            sums[:, SCALAR_QUESTIONS:],
+            prod[:, SCALAR_QUESTIONS * Q :].rearrange("c (b q) -> c b q", q=Q),
+            INNERMOST,
+            ADD,
+        )
 
         state = held.tile([C, B], BF16, name="state")
         nc.vector.tensor_scalar_add(state[:], sums[:], readout[:, 0:1])

@@ -14,15 +14,13 @@ B = 128
 Q = 20
 N = B * Q
 
-PIECE_STARTS = (0, 320, 640, 1280, N)
-PIECES = len(PIECE_STARTS) - 1
-
-SCALAR_QUESTIONS = 48
+PIECES = 4
+PIECE = N // PIECES
+PIECE_QUESTIONS = B // PIECES
 
 BLOCK = 128
-BLOCKS = S // BLOCK
 BLOCKS_IN_BANK = 4
-BANKS = BLOCKS // BLOCKS_IN_BANK
+BANKS = S // (BLOCK * BLOCKS_IN_BANK)
 
 FLOPS = 2 * C * S * B
 
@@ -36,50 +34,43 @@ def tile_memn2n_ss_kernel(tc, x, pe, mem, w, offs, out):
     ):
         offsets = held.tile([C, N // 16], U16, name="offsets")
         nc.sync.dma_start(offsets[:], offs)
-        pe_pieces = []
-        for i in range(PIECES):
-            pe_pieces.append(held.tile([C, PIECE_STARTS[i + 1] - PIECE_STARTS[i]], F32, name=f"pe_piece{i}"))
-        nc.sync.dma_start(pe_pieces[0][:], pe[:, PIECE_STARTS[0] : PIECE_STARTS[1]])
         table = held.tile([C, S], F32, name="table")
         nc.sync.dma_start(table[:, : S // 2], x[:, : S // 2])
-        nc.sync.dma_start(table[:, S // 2 :], x[:, S // 2 :])
-        for i in range(1, PIECES):
-            nc.sync.dma_start(pe_pieces[i][:], pe[:, PIECE_STARTS[i] : PIECE_STARTS[i + 1]])
-        weights = held.tile([C, S], BF16, name="weights")
-        nc.sync.dma_start(weights[:], w)
+        nc.scalar.dma_start(table[:, S // 2 :], x[:, S // 2 :])
+        pe_pieces = []
+        for i in range(PIECES):
+            pe_piece = held.tile([C, PIECE], F32, name=f"pe_piece{i}")
+            queue = nc.sync if i % 2 == 0 else nc.scalar
+            queue.dma_start(pe_piece[:], pe[:, i * PIECE : (i + 1) * PIECE])
+            pe_pieces.append(pe_piece)
         readout = held.tile([C, 1], F32, name="readout")
         nc.sync.dma_start(readout[:], mem)
-
-        prod = held.tile([C, N], F32, name="prod")
-        for i in range(PIECES):
-            first, end = PIECE_STARTS[i], PIECE_STARTS[i + 1]
-            nc.vector.tensor_tensor(
-                prod[:, first:end], table[:].indirect(offsets[:, first // 16 : end // 16]), pe_pieces[i][:], MULT
-            )
+        weights = held.tile([C, S], BF16, name="weights")
+        nc.scalar.dma_start(weights[:], w)
 
         sums = held.tile([C, B], F32, name="sums")
-        unused = held.tile([C, Q], F32, name="unused")
-        for b in range(SCALAR_QUESTIONS):
-            nc.scalar.activation(unused[:], prod[:, b * Q : (b + 1) * Q], COPY, accum_out=sums[:, b : b + 1])
-        nc.vector.tensor_reduce(
-            sums[:, SCALAR_QUESTIONS:],
-            prod[:, SCALAR_QUESTIONS * Q :].rearrange("c (b q) -> c b q", q=Q),
-            INNERMOST,
-            ADD,
-        )
+        for i in range(PIECES):
+            prod = held.tile([C, PIECE], F32, name=f"prod{i}")
+            piece_offsets = offsets[:, i * PIECE // 16 : (i + 1) * PIECE // 16]
+            nc.vector.tensor_tensor(prod[:], table[:].indirect(piece_offsets), pe_pieces[i][:], MULT)
+            nc.vector.tensor_reduce(
+                sums[:, i * PIECE_QUESTIONS : (i + 1) * PIECE_QUESTIONS],
+                prod[:].rearrange("c (b q) -> c b q", q=Q),
+                INNERMOST,
+                ADD,
+            )
 
         state = held.tile([C, B], BF16, name="state")
         nc.vector.tensor_scalar_add(state[:], sums[:], readout[:, 0:1])
 
-        weight_blocks = weights[:].rearrange("c (p k) -> c k p", k=BLOCKS)
-        out_blocks = out.rearrange("(p k) b -> p k b", k=BLOCKS)
+        weight_blocks = weights[:].rearrange("c (g p j) -> c g j p", p=BLOCK, j=BLOCKS_IN_BANK)
+        out_banks = out.rearrange("(g p j) b -> g p (j b)", p=BLOCK, j=BLOCKS_IN_BANK)
         for g in range(BANKS):
             bank = banks.tile([BLOCK, BLOCKS_IN_BANK * B], F32, name="bank")
             for j in range(BLOCKS_IN_BANK):
-                k = g * BLOCKS_IN_BANK + j
                 nc.tensor.matmul(
                     bank[:, j * B : (j + 1) * B],
-                    weight_blocks[:, k, :],
+                    weight_blocks[:, g, j, :],
                     state[:],
                     start=True,
                     stop=True,
@@ -89,7 +80,4 @@ def tile_memn2n_ss_kernel(tc, x, pe, mem, w, offs, out):
                 nc.vector.tensor_copy(staged[:], bank[:])
             else:
                 nc.scalar.activation(staged[:], bank[:], COPY)
-            nc.sync.dma_start(
-                out_blocks[:, g * BLOCKS_IN_BANK : (g + 1) * BLOCKS_IN_BANK, :],
-                staged[:].rearrange("p (k b) -> p k b", b=B),
-            )
+            nc.sync.dma_start(out_banks[g], staged[:])

@@ -14,13 +14,15 @@ B = 128
 Q = 20
 N = B * Q
 
-PIECES = 4
-PIECE = N // PIECES
-PIECE_QUESTIONS = B // PIECES
+PIECE_STARTS = (0, 320, 640, 1280, N)
+PIECES = len(PIECE_STARTS) - 1
+
+SCALAR_QUESTIONS = 48
 
 BLOCK = 128
+BLOCKS = S // BLOCK
 BLOCKS_IN_BANK = 4
-BANKS = S // (BLOCK * BLOCKS_IN_BANK)
+BANKS = BLOCKS // BLOCKS_IN_BANK
 
 FLOPS = 2 * C * S * B
 
@@ -34,43 +36,52 @@ def tile_memn2n_ss_kernel(tc, x, pe, mem, w, offs, out):
     ):
         offsets = held.tile([C, N // 16], U16, name="offsets")
         nc.sync.dma_start(offsets[:], offs)
+        pe_pieces = []
+        for i in range(PIECES):
+            pe_pieces.append(held.tile([C, PIECE_STARTS[i + 1] - PIECE_STARTS[i]], F32, name=f"pe_piece{i}"))
+        nc.scalar.dma_start(pe_pieces[0][:], pe[:, PIECE_STARTS[0] : PIECE_STARTS[1]])
         table = held.tile([C, S], F32, name="table")
         nc.sync.dma_start(table[:, : S // 2], x[:, : S // 2])
         nc.scalar.dma_start(table[:, S // 2 :], x[:, S // 2 :])
-        pe_pieces = []
-        for i in range(PIECES):
-            pe_piece = held.tile([C, PIECE], F32, name=f"pe_piece{i}")
-            queue = nc.sync if i % 2 == 0 else nc.scalar
-            queue.dma_start(pe_piece[:], pe[:, i * PIECE : (i + 1) * PIECE])
-            pe_pieces.append(pe_piece)
-        readout = held.tile([C, 1], F32, name="readout")
-        nc.sync.dma_start(readout[:], mem)
+        nc.sync.dma_start(pe_pieces[1][:], pe[:, PIECE_STARTS[1] : PIECE_STARTS[2]])
+        nc.scalar.dma_start(pe_pieces[2][:], pe[:, PIECE_STARTS[2] : PIECE_STARTS[3]])
+        nc.sync.dma_start(pe_pieces[3][:], pe[:, PIECE_STARTS[3] : PIECE_STARTS[4]])
         weights = held.tile([C, S], BF16, name="weights")
         nc.scalar.dma_start(weights[:], w)
+        readout = held.tile([C, 1], F32, name="readout")
+        nc.sync.dma_start(readout[:], mem)
+
+        prod = held.tile([C, N], F32, name="prod")
+        for i in range(PIECES):
+            first, end = PIECE_STARTS[i], PIECE_STARTS[i + 1]
+            nc.vector.tensor_tensor(
+                prod[:, first:end], table[:].indirect(offsets[:, first // 16 : end // 16]), pe_pieces[i][:], MULT
+            )
 
         sums = held.tile([C, B], F32, name="sums")
-        for i in range(PIECES):
-            prod = held.tile([C, PIECE], F32, name=f"prod{i}")
-            piece_offsets = offsets[:, i * PIECE // 16 : (i + 1) * PIECE // 16]
-            nc.vector.tensor_tensor(prod[:], table[:].indirect(piece_offsets), pe_pieces[i][:], MULT)
-            nc.vector.tensor_reduce(
-                sums[:, i * PIECE_QUESTIONS : (i + 1) * PIECE_QUESTIONS],
-                prod[:].rearrange("c (b q) -> c b q", q=Q),
-                INNERMOST,
-                ADD,
-            )
+        copied = held.tile([C, SCALAR_QUESTIONS * Q], F32, name="copied")
+        for b in range(SCALAR_QUESTIONS):
+            words = slice(b * Q, (b + 1) * Q)
+            nc.scalar.activation(copied[:, words], prod[:, words], COPY, accum_out=sums[:, b : b + 1])
+        nc.vector.tensor_reduce(
+            sums[:, SCALAR_QUESTIONS:],
+            prod[:, SCALAR_QUESTIONS * Q :].rearrange("c (b q) -> c b q", q=Q),
+            INNERMOST,
+            ADD,
+        )
 
         state = held.tile([C, B], BF16, name="state")
         nc.vector.tensor_scalar_add(state[:], sums[:], readout[:, 0:1])
 
-        weight_blocks = weights[:].rearrange("c (g p j) -> c g j p", p=BLOCK, j=BLOCKS_IN_BANK)
-        out_banks = out.rearrange("(g p j) b -> g p (j b)", p=BLOCK, j=BLOCKS_IN_BANK)
+        weight_blocks = weights[:].rearrange("c (p k) -> c k p", k=BLOCKS)
+        out_blocks = out.rearrange("(p k) b -> p k b", k=BLOCKS)
         for g in range(BANKS):
             bank = banks.tile([BLOCK, BLOCKS_IN_BANK * B], F32, name="bank")
             for j in range(BLOCKS_IN_BANK):
+                k = g * BLOCKS_IN_BANK + j
                 nc.tensor.matmul(
                     bank[:, j * B : (j + 1) * B],
-                    weight_blocks[:, g, j, :],
+                    weight_blocks[:, k, :],
                     state[:],
                     start=True,
                     stop=True,
@@ -80,4 +91,7 @@ def tile_memn2n_ss_kernel(tc, x, pe, mem, w, offs, out):
                 nc.vector.tensor_copy(staged[:], bank[:])
             else:
                 nc.scalar.activation(staged[:], bank[:], COPY)
-            nc.sync.dma_start(out_banks[g], staged[:])
+            nc.sync.dma_start(
+                out_blocks[:, g * BLOCKS_IN_BANK : (g + 1) * BLOCKS_IN_BANK, :],
+                staged[:].rearrange("p (k b) -> p k b", b=B),
+            )

@@ -17,7 +17,7 @@ N = B * Q
 PIECE_STARTS = (0, 320, 640, 1280, N)
 PIECES = len(PIECE_STARTS) - 1
 
-SCALAR_QUESTIONS = 48
+SCALAR_QUESTIONS = 40
 
 BLOCK = 128
 BLOCKS = S // BLOCK

@@ -14,15 +14,14 @@ B = 128
 Q = 20
 N = B * Q
 
-PIECE_STARTS = (0, 320, 640, 1280, N)
-PIECES = len(PIECE_STARTS) - 1
+PIECES = 4
+PIECE = N // PIECES
 
-SCALAR_QUESTIONS = 40
+SCALAR_QUESTIONS = B // 2
 
 BLOCK = 128
-BLOCKS = S // BLOCK
 BLOCKS_IN_BANK = 4
-BANKS = BLOCKS // BLOCKS_IN_BANK
+BANKS = S // (BLOCK * BLOCKS_IN_BANK)
 
 FLOPS = 2 * C * S * B
 
@@ -36,27 +35,25 @@ def tile_memn2n_ss_kernel(tc, x, pe, mem, w, offs, out):
     ):
         offsets = held.tile([C, N // 16], U16, name="offsets")
         nc.sync.dma_start(offsets[:], offs)
-        pe_pieces = []
-        for i in range(PIECES):
-            pe_pieces.append(held.tile([C, PIECE_STARTS[i + 1] - PIECE_STARTS[i]], F32, name=f"pe_piece{i}"))
-        nc.scalar.dma_start(pe_pieces[0][:], pe[:, PIECE_STARTS[0] : PIECE_STARTS[1]])
         table = held.tile([C, S], F32, name="table")
         nc.sync.dma_start(table[:, : S // 2], x[:, : S // 2])
         nc.scalar.dma_start(table[:, S // 2 :], x[:, S // 2 :])
-        nc.sync.dma_start(pe_pieces[1][:], pe[:, PIECE_STARTS[1] : PIECE_STARTS[2]])
-        nc.scalar.dma_start(pe_pieces[2][:], pe[:, PIECE_STARTS[2] : PIECE_STARTS[3]])
-        nc.sync.dma_start(pe_pieces[3][:], pe[:, PIECE_STARTS[3] : PIECE_STARTS[4]])
-        weights = held.tile([C, S], BF16, name="weights")
-        nc.scalar.dma_start(weights[:], w)
+        pe_pieces = []
+        for i in range(PIECES):
+            pe_piece = held.tile([C, PIECE], F32, name=f"pe_piece{i}")
+            queue = nc.sync if i % 2 == 0 else nc.scalar
+            queue.dma_start(pe_piece[:], pe[:, i * PIECE : (i + 1) * PIECE])
+            pe_pieces.append(pe_piece)
         readout = held.tile([C, 1], F32, name="readout")
         nc.sync.dma_start(readout[:], mem)
+        weights = held.tile([C, S], BF16, name="weights")
+        nc.scalar.dma_start(weights[:], w)
 
         prod = held.tile([C, N], F32, name="prod")
         for i in range(PIECES):
-            first, end = PIECE_STARTS[i], PIECE_STARTS[i + 1]
-            nc.vector.tensor_tensor(
-                prod[:, first:end], table[:].indirect(offsets[:, first // 16 : end // 16]), pe_pieces[i][:], MULT
-            )
+            entries = slice(i * PIECE, (i + 1) * PIECE)
+            piece_offsets = offsets[:, i * PIECE // 16 : (i + 1) * PIECE // 16]
+            nc.vector.tensor_tensor(prod[:, entries], table[:].indirect(piece_offsets), pe_pieces[i][:], MULT)
 
         sums = held.tile([C, B], F32, name="sums")
         copied = held.tile([C, SCALAR_QUESTIONS * Q], F32, name="copied")
@@ -73,15 +70,14 @@ def tile_memn2n_ss_kernel(tc, x, pe, mem, w, offs, out):
         state = held.tile([C, B], BF16, name="state")
         nc.vector.tensor_scalar_add(state[:], sums[:], readout[:, 0:1])
 
-        weight_blocks = weights[:].rearrange("c (p k) -> c k p", k=BLOCKS)
-        out_blocks = out.rearrange("(p k) b -> p k b", k=BLOCKS)
+        weight_blocks = weights[:].rearrange("c (g p j) -> c g j p", p=BLOCK, j=BLOCKS_IN_BANK)
+        out_banks = out.rearrange("(g p j) b -> g p (j b)", p=BLOCK, j=BLOCKS_IN_BANK)
         for g in range(BANKS):
             bank = banks.tile([BLOCK, BLOCKS_IN_BANK * B], F32, name="bank")
             for j in range(BLOCKS_IN_BANK):
-                k = g * BLOCKS_IN_BANK + j
                 nc.tensor.matmul(
                     bank[:, j * B : (j + 1) * B],
-                    weight_blocks[:, k, :],
+                    weight_blocks[:, g, j, :],
                     state[:],
                     start=True,
                     stop=True,
@@ -91,7 +87,4 @@ def tile_memn2n_ss_kernel(tc, x, pe, mem, w, offs, out):
                 nc.vector.tensor_copy(staged[:], bank[:])
             else:
                 nc.scalar.activation(staged[:], bank[:], COPY)
-            nc.sync.dma_start(
-                out_blocks[:, g * BLOCKS_IN_BANK : (g + 1) * BLOCKS_IN_BANK, :],
-                staged[:].rearrange("p (k b) -> p k b", b=B),
-            )
+            nc.sync.dma_start(out_banks[g], staged[:])

@@ -17,7 +17,7 @@ N = B * Q
 PIECES = 4
 PIECE = N // PIECES
 
-SCALAR_QUESTIONS = B // 2
+SCALAR_QUESTIONS = 3 * B // 8
 
 BLOCK = 128
 BLOCKS_IN_BANK = 4

@@ -14,8 +14,9 @@ B = 128
 Q = 20
 N = B * Q
 
-PIECES = 4
-PIECE = N // PIECES
+PIECE_QUESTIONS = [8, 16, 32, 72]
+assert sum(PIECE_QUESTIONS) == B
+PIECE_STARTS = [Q * sum(PIECE_QUESTIONS[:i]) for i in range(len(PIECE_QUESTIONS) + 1)]
 
 SCALAR_QUESTIONS = 3 * B // 8
 
@@ -38,21 +39,20 @@ def tile_memn2n_ss_kernel(tc, x, pe, mem, w, offs, out):
         table = held.tile([C, S], F32, name="table")
         nc.sync.dma_start(table[:, : S // 2], x[:, : S // 2])
         nc.scalar.dma_start(table[:, S // 2 :], x[:, S // 2 :])
-        pe_pieces = []
-        for i in range(PIECES):
-            pe_piece = held.tile([C, PIECE], F32, name=f"pe_piece{i}")
-            queue = nc.sync if i % 2 == 0 else nc.scalar
-            queue.dma_start(pe_piece[:], pe[:, i * PIECE : (i + 1) * PIECE])
-            pe_pieces.append(pe_piece)
         readout = held.tile([C, 1], F32, name="readout")
-        nc.sync.dma_start(readout[:], mem)
+        nc.scalar.dma_start(readout[:], mem)
+        pe_pieces = []
+        for i in range(len(PIECE_QUESTIONS)):
+            pe_piece = held.tile([C, Q * PIECE_QUESTIONS[i]], F32, name=f"pe_piece{i}")
+            nc.sync.dma_start(pe_piece[:], pe[:, PIECE_STARTS[i] : PIECE_STARTS[i + 1]])
+            pe_pieces.append(pe_piece)
         weights = held.tile([C, S], BF16, name="weights")
-        nc.scalar.dma_start(weights[:], w)
+        nc.sync.dma_start(weights[:], w)
 
         prod = held.tile([C, N], F32, name="prod")
-        for i in range(PIECES):
-            entries = slice(i * PIECE, (i + 1) * PIECE)
-            piece_offsets = offsets[:, i * PIECE // 16 : (i + 1) * PIECE // 16]
+        for i in range(len(PIECE_QUESTIONS)):
+            entries = slice(PIECE_STARTS[i], PIECE_STARTS[i + 1])
+            piece_offsets = offsets[:, PIECE_STARTS[i] // 16 : PIECE_STARTS[i + 1] // 16]
             nc.vector.tensor_tensor(prod[:, entries], table[:].indirect(piece_offsets), pe_pieces[i][:], MULT)
 
         sums = held.tile([C, B], F32, name="sums")

@@ -21,8 +21,10 @@ PIECE_STARTS = [Q * sum(PIECE_QUESTIONS[:i]) for i in range(len(PIECE_QUESTIONS)
 SCALAR_QUESTIONS = 3 * B // 8
 
 BLOCK = 128
-BLOCKS_IN_BANK = 4
-BANKS = S // (BLOCK * BLOCKS_IN_BANK)
+BLOCKS_IN_GROUP = 4
+BLOCKS_IN_HALF = BLOCKS_IN_GROUP // 2
+GROUPS = S // (BLOCK * BLOCKS_IN_GROUP)
+PSUM_BANKS = 8
 
 FLOPS = 2 * C * S * B
 
@@ -31,8 +33,8 @@ def tile_memn2n_ss_kernel(tc, x, pe, mem, w, offs, out):
     nc = tc.nc
     with (
         tc.tile_pool(name="held", bufs=1) as held,
-        tc.tile_pool(name="staging", bufs=BANKS) as staging,
-        tc.psum_pool(name="banks", bufs=BANKS) as banks,
+        tc.tile_pool(name="staging", bufs=GROUPS) as staging,
+        tc.psum_pool(name="halves", bufs=PSUM_BANKS) as halves,
     ):
         offsets = held.tile([C, N // 16], U16, name="offsets")
         nc.sync.dma_start(offsets[:], offs)
@@ -70,21 +72,23 @@ def tile_memn2n_ss_kernel(tc, x, pe, mem, w, offs, out):
         state = held.tile([C, B], BF16, name="state")
         nc.vector.tensor_scalar_add(state[:], sums[:], readout[:, 0:1])
 
-        weight_blocks = weights[:].rearrange("c (g p j) -> c g j p", p=BLOCK, j=BLOCKS_IN_BANK)
-        out_banks = out.rearrange("(g p j) b -> g p (j b)", p=BLOCK, j=BLOCKS_IN_BANK)
-        for g in range(BANKS):
-            bank = banks.tile([BLOCK, BLOCKS_IN_BANK * B], F32, name="bank")
-            for j in range(BLOCKS_IN_BANK):
-                nc.tensor.matmul(
-                    bank[:, j * B : (j + 1) * B],
-                    weight_blocks[:, g, j, :],
-                    state[:],
-                    start=True,
-                    stop=True,
-                )
-            staged = staging.tile([BLOCK, BLOCKS_IN_BANK * B], F32, name="staged")
-            if g % 2 == 0:
-                nc.vector.tensor_copy(staged[:], bank[:])
-            else:
-                nc.scalar.activation(staged[:], bank[:], COPY)
-            nc.sync.dma_start(out_banks[g], staged[:])
+        weight_blocks = weights[:].rearrange("c (g p j) -> c g j p", p=BLOCK, j=BLOCKS_IN_GROUP)
+        out_groups = out.rearrange("(g p j) b -> g p (j b)", p=BLOCK, j=BLOCKS_IN_GROUP)
+        for g in range(GROUPS):
+            staged = staging.tile([BLOCK, BLOCKS_IN_GROUP * B], F32, name="staged")
+            for h in range(2):
+                half = halves.tile([BLOCK, BLOCKS_IN_HALF * B], F32, name="half")
+                for i in range(BLOCKS_IN_HALF):
+                    nc.tensor.matmul(
+                        half[:, i * B : (i + 1) * B],
+                        weight_blocks[:, g, h * BLOCKS_IN_HALF + i, :],
+                        state[:],
+                        start=True,
+                        stop=True,
+                    )
+                staged_half = staged[:, h * BLOCKS_IN_HALF * B : (h + 1) * BLOCKS_IN_HALF * B]
+                if h == 0:
+                    nc.vector.tensor_copy(staged_half, half[:])
+                else:
+                    nc.scalar.activation(staged_half, half[:], COPY)
+            nc.sync.dma_start(out_groups[g], staged[:])

@@ -14,7 +14,7 @@ B = 128
 Q = 20
 N = B * Q
 
-PIECE_QUESTIONS = [8, 16, 32, 72]
+PIECE_QUESTIONS = [8, 16, 32, 32, 40]
 assert sum(PIECE_QUESTIONS) == B
 PIECE_STARTS = [Q * sum(PIECE_QUESTIONS[:i]) for i in range(len(PIECE_QUESTIONS) + 1)]
 

@@ -18,7 +18,7 @@ PIECE_QUESTIONS = [8, 16, 32, 32, 40]
 assert sum(PIECE_QUESTIONS) == B
 PIECE_STARTS = [Q * sum(PIECE_QUESTIONS[:i]) for i in range(len(PIECE_QUESTIONS) + 1)]
 
-SCALAR_QUESTIONS = 3 * B // 8
+SCALAR_QUESTIONS = sum(PIECE_QUESTIONS[:3])
 
 BLOCK = 128
 BLOCKS_IN_GROUP = 4

@@ -6,6 +6,7 @@ U16 = mybir.dt.uint16
 MULT = mybir.AluOpType.mult
 ADD = mybir.AluOpType.add
 COPY = mybir.ActivationFunctionType.Copy
+IDENTITY = mybir.ActivationFunctionType.Identity
 INNERMOST = mybir.AxisListType.X
 
 C = 128
@@ -70,25 +71,25 @@ def tile_memn2n_ss_kernel(tc, x, pe, mem, w, offs, out):
         )
 
         state = held.tile([C, B], BF16, name="state")
-        nc.vector.tensor_scalar_add(state[:], sums[:], readout[:, 0:1])
+        nc.scalar.activation(state[:, :SCALAR_QUESTIONS], sums[:, :SCALAR_QUESTIONS], IDENTITY, bias=readout[:, 0:1])
+        nc.vector.tensor_scalar_add(state[:, SCALAR_QUESTIONS:], sums[:, SCALAR_QUESTIONS:], readout[:, 0:1])
 
         weight_blocks = weights[:].rearrange("c (g p j) -> c g j p", p=BLOCK, j=BLOCKS_IN_GROUP)
         out_groups = out.rearrange("(g p j) b -> g p (j b)", p=BLOCK, j=BLOCKS_IN_GROUP)
+        column_ranges = ((0, SCALAR_QUESTIONS), (SCALAR_QUESTIONS, B))
         for g in range(GROUPS):
             staged = staging.tile([BLOCK, BLOCKS_IN_GROUP * B], F32, name="staged")
-            for h in range(2):
-                half = halves.tile([BLOCK, BLOCKS_IN_HALF * B], F32, name="half")
-                for i in range(BLOCKS_IN_HALF):
+            group_halves = [halves.tile([BLOCK, BLOCKS_IN_HALF * B], F32, name="half") for h in range(2)]
+            for first, end in column_ranges:
+                for j in range(BLOCKS_IN_GROUP):
+                    i = j % BLOCKS_IN_HALF
                     nc.tensor.matmul(
-                        half[:, i * B : (i + 1) * B],
-                        weight_blocks[:, g, h * BLOCKS_IN_HALF + i, :],
-                        state[:],
+                        group_halves[j // BLOCKS_IN_HALF][:, i * B + first : i * B + end],
+                        weight_blocks[:, g, j, :],
+                        state[:, first:end],
                         start=True,
                         stop=True,
                     )
-                staged_half = staged[:, h * BLOCKS_IN_HALF * B : (h + 1) * BLOCKS_IN_HALF * B]
-                if h == 0:
-                    nc.vector.tensor_copy(staged_half, half[:])
-                else:
-                    nc.scalar.activation(staged_half, half[:], COPY)
+            nc.vector.tensor_copy(staged[:, : BLOCKS_IN_HALF * B], group_halves[0][:])
+            nc.scalar.activation(staged[:, BLOCKS_IN_HALF * B :], group_halves[1][:], COPY)
             nc.sync.dma_start(out_groups[g], staged[:])

@@ -76,8 +76,8 @@ def tile_memn2n_ss_kernel(tc, x, pe, mem, w, offs, out):
 
         weight_blocks = weights[:].rearrange("c (g p j) -> c g j p", p=BLOCK, j=BLOCKS_IN_GROUP)
         out_groups = out.rearrange("(g p j) b -> g p (j b)", p=BLOCK, j=BLOCKS_IN_GROUP)
-        column_ranges = ((0, SCALAR_QUESTIONS), (SCALAR_QUESTIONS, B))
         for g in range(GROUPS):
+            column_ranges = ((0, SCALAR_QUESTIONS), (SCALAR_QUESTIONS, B)) if g == 0 else ((0, B),)
             staged = staging.tile([BLOCK, BLOCKS_IN_GROUP * B], F32, name="staged")
             group_halves = [halves.tile([BLOCK, BLOCKS_IN_HALF * B], F32, name="half") for h in range(2)]
             for first, end in column_ranges:

@@ -26,6 +26,8 @@ BLOCKS_IN_GROUP = 4
 BLOCKS_IN_HALF = BLOCKS_IN_GROUP // 2
 GROUPS = S // (BLOCK * BLOCKS_IN_GROUP)
 PSUM_BANKS = 8
+GROUPS_IN_STORE = [1, 1, 1, 1, 2, 2]
+assert sum(GROUPS_IN_STORE) == GROUPS
 
 FLOPS = 2 * C * S * B
 
@@ -34,7 +36,7 @@ def tile_memn2n_ss_kernel(tc, x, pe, mem, w, offs, out):
     nc = tc.nc
     with (
         tc.tile_pool(name="held", bufs=1) as held,
-        tc.tile_pool(name="staging", bufs=GROUPS) as staging,
+        tc.tile_pool(name="staging", bufs=max(GROUPS_IN_STORE.count(n) for n in GROUPS_IN_STORE)) as staging,
         tc.psum_pool(name="halves", bufs=PSUM_BANKS) as halves,
     ):
         offsets = held.tile([C, N // 16], U16, name="offsets")
@@ -75,21 +77,27 @@ def tile_memn2n_ss_kernel(tc, x, pe, mem, w, offs, out):
         nc.vector.tensor_scalar_add(state[:, SCALAR_QUESTIONS:], sums[:, SCALAR_QUESTIONS:], readout[:, 0:1])
 
         weight_blocks = weights[:].rearrange("c (g p j) -> c g j p", p=BLOCK, j=BLOCKS_IN_GROUP)
-        out_groups = out.rearrange("(g p j) b -> g p (j b)", p=BLOCK, j=BLOCKS_IN_GROUP)
-        for g in range(GROUPS):
-            column_ranges = ((0, SCALAR_QUESTIONS), (SCALAR_QUESTIONS, B)) if g == 0 else ((0, B),)
-            staged = staging.tile([BLOCK, BLOCKS_IN_GROUP * B], F32, name="staged")
-            group_halves = [halves.tile([BLOCK, BLOCKS_IN_HALF * B], F32, name="half") for h in range(2)]
-            for first, end in column_ranges:
-                for j in range(BLOCKS_IN_GROUP):
-                    i = j % BLOCKS_IN_HALF
-                    nc.tensor.matmul(
-                        group_halves[j // BLOCKS_IN_HALF][:, i * B + first : i * B + end],
-                        weight_blocks[:, g, j, :],
-                        state[:, first:end],
-                        start=True,
-                        stop=True,
-                    )
-            nc.vector.tensor_copy(staged[:, : BLOCKS_IN_HALF * B], group_halves[0][:])
-            nc.scalar.activation(staged[:, BLOCKS_IN_HALF * B :], group_halves[1][:], COPY)
-            nc.sync.dma_start(out_groups[g], staged[:])
+        out_groups = out.rearrange("(g p j) b -> p g (j b)", p=BLOCK, j=BLOCKS_IN_GROUP)
+        first_group = 0
+        for groups_in_store in GROUPS_IN_STORE:
+            staged = staging.tile(
+                [BLOCK, groups_in_store, BLOCKS_IN_GROUP * B], F32, name=f"staged{groups_in_store}"
+            )
+            for k in range(groups_in_store):
+                g = first_group + k
+                column_ranges = ((0, SCALAR_QUESTIONS), (SCALAR_QUESTIONS, B)) if g == 0 else ((0, B),)
+                group_halves = [halves.tile([BLOCK, BLOCKS_IN_HALF * B], F32, name="half") for h in range(2)]
+                for first, end in column_ranges:
+                    for j in range(BLOCKS_IN_GROUP):
+                        i = j % BLOCKS_IN_HALF
+                        nc.tensor.matmul(
+                            group_halves[j // BLOCKS_IN_HALF][:, i * B + first : i * B + end],
+                            weight_blocks[:, g, j, :],
+                            state[:, first:end],
+                            start=True,
+                            stop=True,
+                        )
+                nc.vector.tensor_copy(staged[:, k, : BLOCKS_IN_HALF * B], group_halves[0][:])
+                nc.scalar.activation(staged[:, k, BLOCKS_IN_HALF * B :], group_halves[1][:], COPY)
+            nc.sync.dma_start(out_groups[:, first_group : first_group + groups_in_store, :], staged[:])
+            first_group += groups_in_store

@@ -15,11 +15,12 @@ B = 128
 Q = 20
 N = B * Q
 
-PIECE_QUESTIONS = [8, 16, 32, 32, 40]
+PIECE_QUESTIONS = [8, 16, 24, 48, 32]
 assert sum(PIECE_QUESTIONS) == B
 PIECE_STARTS = [Q * sum(PIECE_QUESTIONS[:i]) for i in range(len(PIECE_QUESTIONS) + 1)]
 
 SCALAR_QUESTIONS = sum(PIECE_QUESTIONS[:3])
+LAST_START = B - PIECE_QUESTIONS[-1]
 
 BLOCK = 128
 BLOCKS_IN_GROUP = 4
@@ -65,21 +66,28 @@ def tile_memn2n_ss_kernel(tc, x, pe, mem, w, offs, out):
         for b in range(SCALAR_QUESTIONS):
             words = slice(b * Q, (b + 1) * Q)
             nc.scalar.activation(copied[:, words], prod[:, words], COPY, accum_out=sums[:, b : b + 1])
-        nc.vector.tensor_reduce(
-            sums[:, SCALAR_QUESTIONS:],
-            prod[:, SCALAR_QUESTIONS * Q :].rearrange("c (b q) -> c b q", q=Q),
-            INNERMOST,
+        words_by_question = prod[:].rearrange("c (b q) -> c b q", q=Q)
+        half_sums = held.tile([C, B - LAST_START, Q // 2], F32, name="half_sums")
+        nc.gpsimd.tensor_tensor(
+            half_sums[:],
+            words_by_question[:, LAST_START:, : Q // 2],
+            words_by_question[:, LAST_START:, Q // 2 :],
             ADD,
         )
+        nc.vector.tensor_reduce(
+            sums[:, SCALAR_QUESTIONS:LAST_START], words_by_question[:, SCALAR_QUESTIONS:LAST_START, :], INNERMOST, ADD
+        )
+        nc.vector.tensor_reduce(sums[:, LAST_START:], half_sums[:], INNERMOST, ADD)
 
         state = held.tile([C, B], BF16, name="state")
         nc.scalar.activation(state[:, :SCALAR_QUESTIONS], sums[:, :SCALAR_QUESTIONS], IDENTITY, bias=readout[:, 0:1])
         nc.vector.tensor_scalar_add(state[:, SCALAR_QUESTIONS:], sums[:, SCALAR_QUESTIONS:], readout[:, 0:1])
 
-        weight_blocks = weights[:].rearrange("c (g p j) -> c g j p", p=BLOCK, j=BLOCKS_IN_GROUP)
-        out_groups = out.rearrange("(g p j) b -> p g (j b)", p=BLOCK, j=BLOCKS_IN_GROUP)
         first_group = 0
         for groups_in_store in GROUPS_IN_STORE:
+            blocks_in_store = groups_in_store * BLOCKS_IN_GROUP
+            words = slice(first_group * BLOCKS_IN_GROUP * BLOCK, (first_group + groups_in_store) * BLOCKS_IN_GROUP * BLOCK)
+            weight_blocks = weights[:, words].rearrange("c (p j) -> c j p", j=blocks_in_store)
             staged = staging.tile(
                 [BLOCK, groups_in_store, BLOCKS_IN_GROUP * B], F32, name=f"staged{groups_in_store}"
             )
@@ -92,12 +100,15 @@ def tile_memn2n_ss_kernel(tc, x, pe, mem, w, offs, out):
                         i = j % BLOCKS_IN_HALF
                         nc.tensor.matmul(
                             group_halves[j // BLOCKS_IN_HALF][:, i * B + first : i * B + end],
-                            weight_blocks[:, g, j, :],
+                            weight_blocks[:, k * BLOCKS_IN_GROUP + j, :],
                             state[:, first:end],
                             start=True,
                             stop=True,
                         )
                 nc.vector.tensor_copy(staged[:, k, : BLOCKS_IN_HALF * B], group_halves[0][:])
                 nc.scalar.activation(staged[:, k, BLOCKS_IN_HALF * B :], group_halves[1][:], COPY)
-            nc.sync.dma_start(out_groups[:, first_group : first_group + groups_in_store, :], staged[:])
+            nc.sync.dma_start(
+                out[words, :].rearrange("(p j) b -> p (j b)", j=blocks_in_store),
+                staged[:].rearrange("p k n -> p (k n)"),
+            )
             first_group += groups_in_store

@@ -15,7 +15,7 @@ B = 128
 Q = 20
 N = B * Q
 
-PIECE_QUESTIONS = [8, 16, 24, 48, 32]
+PIECE_QUESTIONS = [8, 16, 24, 56, 24]
 assert sum(PIECE_QUESTIONS) == B
 PIECE_STARTS = [Q * sum(PIECE_QUESTIONS[:i]) for i in range(len(PIECE_QUESTIONS) + 1)]
 
@@ -61,15 +61,19 @@ def tile_memn2n_ss_kernel(tc, x, pe, mem, w, offs, out):
             piece_offsets = offsets[:, PIECE_STARTS[i] // 16 : PIECE_STARTS[i + 1] // 16]
             nc.vector.tensor_tensor(prod[:, entries], table[:].indirect(piece_offsets), pe_pieces[i][:], MULT)
 
-        sums = held.tile([C, B], F32, name="sums")
+        half_sums = held.tile([C, B - LAST_START, Q // 2 + 1], F32, name="half_sums")
+        nc.scalar.activation(
+            half_sums[:, :, Q // 2], readout[:, 0:1].to_broadcast([C, B - LAST_START]), COPY
+        )
+
+        sums = held.tile([C, LAST_START], F32, name="sums")
         copied = held.tile([C, SCALAR_QUESTIONS * Q], F32, name="copied")
         for b in range(SCALAR_QUESTIONS):
             words = slice(b * Q, (b + 1) * Q)
             nc.scalar.activation(copied[:, words], prod[:, words], COPY, accum_out=sums[:, b : b + 1])
         words_by_question = prod[:].rearrange("c (b q) -> c b q", q=Q)
-        half_sums = held.tile([C, B - LAST_START, Q // 2], F32, name="half_sums")
         nc.gpsimd.tensor_tensor(
-            half_sums[:],
+            half_sums[:, :, : Q // 2],
             words_by_question[:, LAST_START:, : Q // 2],
             words_by_question[:, LAST_START:, Q // 2 :],
             ADD,
@@ -77,11 +81,14 @@ def tile_memn2n_ss_kernel(tc, x, pe, mem, w, offs, out):
         nc.vector.tensor_reduce(
             sums[:, SCALAR_QUESTIONS:LAST_START], words_by_question[:, SCALAR_QUESTIONS:LAST_START, :], INNERMOST, ADD
         )
-        nc.vector.tensor_reduce(sums[:, LAST_START:], half_sums[:], INNERMOST, ADD)
 
         state = held.tile([C, B], BF16, name="state")
         nc.scalar.activation(state[:, :SCALAR_QUESTIONS], sums[:, :SCALAR_QUESTIONS], IDENTITY, bias=readout[:, 0:1])
-        nc.vector.tensor_scalar_add(state[:, SCALAR_QUESTIONS:], sums[:, SCALAR_QUESTIONS:], readout[:, 0:1])
+        nc.vector.tensor_scalar_add(
+            state[:, SCALAR_QUESTIONS:LAST_START], sums[:, SCALAR_QUESTIONS:LAST_START], readout[:, 0:1]
+        )
+        with nc.allow_low_precision(reason="u is rounded once to bfloat16, as the task asks"):
+            nc.vector.tensor_reduce(state[:, LAST_START:], half_sums[:], INNERMOST, ADD)
 
         first_group = 0
         for groups_in_store in GROUPS_IN_STORE:
@@ -93,7 +100,7 @@ def tile_memn2n_ss_kernel(tc, x, pe, mem, w, offs, out):
             )
             for k in range(groups_in_store):
                 g = first_group + k
-                column_ranges = ((0, SCALAR_QUESTIONS), (SCALAR_QUESTIONS, B)) if g == 0 else ((0, B),)
+                column_ranges = ((0, LAST_START), (LAST_START, B)) if g == 0 else ((0, B),)
                 group_halves = [halves.tile([BLOCK, BLOCKS_IN_HALF * B], F32, name="half") for h in range(2)]
                 for first, end in column_ranges:
                     for j in range(BLOCKS_IN_GROUP):

@@ -84,8 +84,11 @@ def tile_memn2n_ss_kernel(tc, x, pe, mem, w, offs, out):
 
         state = held.tile([C, B], BF16, name="state")
         nc.scalar.activation(state[:, :SCALAR_QUESTIONS], sums[:, :SCALAR_QUESTIONS], IDENTITY, bias=readout[:, 0:1])
-        nc.vector.tensor_scalar_add(
-            state[:, SCALAR_QUESTIONS:LAST_START], sums[:, SCALAR_QUESTIONS:LAST_START], readout[:, 0:1]
+        nc.scalar.activation(
+            state[:, SCALAR_QUESTIONS:LAST_START],
+            sums[:, SCALAR_QUESTIONS:LAST_START],
+            IDENTITY,
+            bias=readout[:, 0:1],
         )
         with nc.allow_low_precision(reason="u is rounded once to bfloat16, as the task asks"):
             nc.vector.tensor_reduce(state[:, LAST_START:], half_sums[:], INNERMOST, ADD)
@@ -100,7 +103,7 @@ def tile_memn2n_ss_kernel(tc, x, pe, mem, w, offs, out):
             )
             for k in range(groups_in_store):
                 g = first_group + k
-                column_ranges = ((0, LAST_START), (LAST_START, B)) if g == 0 else ((0, B),)
+                column_ranges = ((0, SCALAR_QUESTIONS), (SCALAR_QUESTIONS, B)) if g == 0 else ((0, B),)
                 group_halves = [halves.tile([BLOCK, BLOCKS_IN_HALF * B], F32, name="half") for h in range(2)]
                 for first, end in column_ranges:
                     for j in range(BLOCKS_IN_GROUP):

@@ -23,12 +23,10 @@ SCALAR_QUESTIONS = sum(PIECE_QUESTIONS[:3])
 LAST_START = B - PIECE_QUESTIONS[-1]
 
 BLOCK = 128
-BLOCKS_IN_GROUP = 4
-BLOCKS_IN_HALF = BLOCKS_IN_GROUP // 2
-GROUPS = S // (BLOCK * BLOCKS_IN_GROUP)
 PSUM_BANKS = 8
-GROUPS_IN_STORE = [1, 1, 1, 1, 2, 2]
-assert sum(GROUPS_IN_STORE) == GROUPS
+EARLY_BLOCKS = PSUM_BANKS
+BLOCKS_IN_STORE = [2, 2, 4, 4, 4, 4, 4, 8]
+assert sum(BLOCKS_IN_STORE) * BLOCK == S
 
 FLOPS = 2 * C * S * B
 
@@ -37,8 +35,8 @@ def tile_memn2n_ss_kernel(tc, x, pe, mem, w, offs, out):
     nc = tc.nc
     with (
         tc.tile_pool(name="held", bufs=1) as held,
-        tc.tile_pool(name="staging", bufs=max(GROUPS_IN_STORE.count(n) for n in GROUPS_IN_STORE)) as staging,
-        tc.psum_pool(name="halves", bufs=PSUM_BANKS) as halves,
+        tc.tile_pool(name="staging", bufs=max(BLOCKS_IN_STORE.count(n) for n in BLOCKS_IN_STORE)) as staging,
+        tc.psum_pool(name="banks", bufs=PSUM_BANKS) as banks,
     ):
         offsets = held.tile([C, N // 16], U16, name="offsets")
         nc.sync.dma_start(offsets[:], offs)
@@ -93,32 +91,40 @@ def tile_memn2n_ss_kernel(tc, x, pe, mem, w, offs, out):
         with nc.allow_low_precision(reason="u is rounded once to bfloat16, as the task asks"):
             nc.vector.tensor_reduce(state[:, LAST_START:], half_sums[:], INNERMOST, ADD)
 
-        first_group = 0
-        for groups_in_store in GROUPS_IN_STORE:
-            blocks_in_store = groups_in_store * BLOCKS_IN_GROUP
-            words = slice(first_group * BLOCKS_IN_GROUP * BLOCK, (first_group + groups_in_store) * BLOCKS_IN_GROUP * BLOCK)
-            weight_blocks = weights[:, words].rearrange("c (p j) -> c j p", j=blocks_in_store)
-            staged = staging.tile(
-                [BLOCK, groups_in_store, BLOCKS_IN_GROUP * B], F32, name=f"staged{groups_in_store}"
+        stationary = []
+        for blocks_in_store in BLOCKS_IN_STORE:
+            first_word = len(stationary) * BLOCK
+            blocks = weights[:, first_word : first_word + blocks_in_store * BLOCK].rearrange("c (p j) -> c j p", p=BLOCK)
+            for j in range(blocks_in_store):
+                stationary.append(blocks[:, j, :])
+        early_products = []
+        for k in range(EARLY_BLOCKS):
+            product = banks.tile([BLOCK, B], F32, name="product")
+            nc.tensor.matmul(
+                product[:, :SCALAR_QUESTIONS], stationary[k], state[:, :SCALAR_QUESTIONS], start=True, stop=True
             )
-            for k in range(groups_in_store):
-                g = first_group + k
-                column_ranges = ((0, SCALAR_QUESTIONS), (SCALAR_QUESTIONS, B)) if g == 0 else ((0, B),)
-                group_halves = [halves.tile([BLOCK, BLOCKS_IN_HALF * B], F32, name="half") for h in range(2)]
-                for first, end in column_ranges:
-                    for j in range(BLOCKS_IN_GROUP):
-                        i = j % BLOCKS_IN_HALF
-                        nc.tensor.matmul(
-                            group_halves[j // BLOCKS_IN_HALF][:, i * B + first : i * B + end],
-                            weight_blocks[:, k * BLOCKS_IN_GROUP + j, :],
-                            state[:, first:end],
-                            start=True,
-                            stop=True,
-                        )
-                nc.vector.tensor_copy(staged[:, k, : BLOCKS_IN_HALF * B], group_halves[0][:])
-                nc.scalar.activation(staged[:, k, BLOCKS_IN_HALF * B :], group_halves[1][:], COPY)
+            early_products.append(product)
+        first_block = 0
+        for blocks_in_store in BLOCKS_IN_STORE:
+            staged = staging.tile([BLOCK, blocks_in_store, B], F32, name=f"staged{blocks_in_store}")
+            for j in range(blocks_in_store):
+                k = first_block + j
+                if k < EARLY_BLOCKS:
+                    product = early_products[k]
+                    first_column = SCALAR_QUESTIONS
+                else:
+                    product = banks.tile([BLOCK, B], F32, name="product")
+                    first_column = 0
+                nc.tensor.matmul(
+                    product[:, first_column:], stationary[k], state[:, first_column:], start=True, stop=True
+                )
+                if j % 2 == 0:
+                    nc.vector.tensor_copy(staged[:, j, :], product[:])
+                else:
+                    nc.scalar.activation(staged[:, j, :], product[:], COPY)
+            first_word = first_block * BLOCK
             nc.sync.dma_start(
-                out[words, :].rearrange("(p j) b -> p (j b)", j=blocks_in_store),
-                staged[:].rearrange("p k n -> p (k n)"),
+                out[first_word : first_word + blocks_in_store * BLOCK, :].rearrange("(p j) b -> p j b", p=BLOCK),
+                staged[:],
             )
-            first_group += groups_in_store
+            first_block += blocks_in_store

@@ -25,7 +25,7 @@ LAST_START = B - PIECE_QUESTIONS[-1]
 BLOCK = 128
 PSUM_BANKS = 8
 EARLY_BLOCKS = PSUM_BANKS
-BLOCKS_IN_STORE = [2, 2, 4, 4, 4, 4, 4, 8]
+BLOCKS_IN_STORE = [4, 4, 4, 4, 8, 8]
 assert sum(BLOCKS_IN_STORE) * BLOCK == S
 
 FLOPS = 2 * C * S * B

@@ -15,7 +15,7 @@ B = 128
 Q = 20
 N = B * Q
 
-PIECE_QUESTIONS = [8, 16, 24, 56, 24]
+PIECE_QUESTIONS = [8, 16, 32, 48, 24]
 assert sum(PIECE_QUESTIONS) == B
 PIECE_STARTS = [Q * sum(PIECE_QUESTIONS[:i]) for i in range(len(PIECE_QUESTIONS) + 1)]
 

import concourse.mybir as mybir

F32 = mybir.dt.float32
BF16 = mybir.dt.bfloat16
U16 = mybir.dt.uint16
MULT = mybir.AluOpType.mult
ADD = mybir.AluOpType.add
COPY = mybir.ActivationFunctionType.Copy
IDENTITY = mybir.ActivationFunctionType.Identity
INNERMOST = mybir.AxisListType.X

C = 128
S = 4096
B = 128
Q = 20
N = B * Q

PIECE_QUESTIONS = [8, 16, 32, 48, 24]
assert sum(PIECE_QUESTIONS) == B
PIECE_STARTS = [Q * sum(PIECE_QUESTIONS[:i]) for i in range(len(PIECE_QUESTIONS) + 1)]

SCALAR_QUESTIONS = sum(PIECE_QUESTIONS[:3])
LAST_START = B - PIECE_QUESTIONS[-1]

BLOCK = 128
PSUM_BANKS = 8
EARLY_BLOCKS = PSUM_BANKS
BLOCKS_IN_STORE = [4, 4, 4, 4, 8, 8]
assert sum(BLOCKS_IN_STORE) * BLOCK == S

FLOPS = 2 * C * S * B


def tile_memn2n_ss_kernel(tc, x, pe, mem, w, offs, out):
    nc = tc.nc
    with (
        tc.tile_pool(name="held", bufs=1) as held,
        tc.tile_pool(name="staging", bufs=max(BLOCKS_IN_STORE.count(n) for n in BLOCKS_IN_STORE)) as staging,
        tc.psum_pool(name="banks", bufs=PSUM_BANKS) as banks,
    ):
        offsets = held.tile([C, N // 16], U16, name="offsets")
        nc.sync.dma_start(offsets[:], offs)
        table = held.tile([C, S], F32, name="table")
        nc.sync.dma_start(table[:, : S // 2], x[:, : S // 2])
        nc.scalar.dma_start(table[:, S // 2 :], x[:, S // 2 :])
        readout = held.tile([C, 1], F32, name="readout")
        nc.scalar.dma_start(readout[:], mem)
        pe_pieces = []
        for i in range(len(PIECE_QUESTIONS)):
            pe_piece = held.tile([C, Q * PIECE_QUESTIONS[i]], F32, name=f"pe_piece{i}")
            nc.sync.dma_start(pe_piece[:], pe[:, PIECE_STARTS[i] : PIECE_STARTS[i + 1]])
            pe_pieces.append(pe_piece)
        weights = held.tile([C, S], BF16, name="weights")
        nc.sync.dma_start(weights[:], w)

        prod = held.tile([C, N], F32, name="prod")
        for i in range(len(PIECE_QUESTIONS)):
            entries = slice(PIECE_STARTS[i], PIECE_STARTS[i + 1])
            piece_offsets = offsets[:, PIECE_STARTS[i] // 16 : PIECE_STARTS[i + 1] // 16]
            nc.vector.tensor_tensor(prod[:, entries], table[:].indirect(piece_offsets), pe_pieces[i][:], MULT)

        half_sums = held.tile([C, B - LAST_START, Q // 2 + 1], F32, name="half_sums")
        nc.scalar.activation(
            half_sums[:, :, Q // 2], readout[:, 0:1].to_broadcast([C, B - LAST_START]), COPY
        )

        sums = held.tile([C, LAST_START], F32, name="sums")
        copied = held.tile([C, SCALAR_QUESTIONS * Q], F32, name="copied")
        for b in range(SCALAR_QUESTIONS):
            words = slice(b * Q, (b + 1) * Q)
            nc.scalar.activation(copied[:, words], prod[:, words], COPY, accum_out=sums[:, b : b + 1])
        words_by_question = prod[:].rearrange("c (b q) -> c b q", q=Q)
        nc.gpsimd.tensor_tensor(
            half_sums[:, :, : Q // 2],
            words_by_question[:, LAST_START:, : Q // 2],
            words_by_question[:, LAST_START:, Q // 2 :],
            ADD,
        )
        nc.vector.tensor_reduce(
            sums[:, SCALAR_QUESTIONS:LAST_START], words_by_question[:, SCALAR_QUESTIONS:LAST_START, :], INNERMOST, ADD
        )

        state = held.tile([C, B], BF16, name="state")
        nc.scalar.activation(state[:, :SCALAR_QUESTIONS], sums[:, :SCALAR_QUESTIONS], IDENTITY, bias=readout[:, 0:1])
        nc.scalar.activation(
            state[:, SCALAR_QUESTIONS:LAST_START],
            sums[:, SCALAR_QUESTIONS:LAST_START],
            IDENTITY,
            bias=readout[:, 0:1],
        )
        with nc.allow_low_precision(reason="u is rounded once to bfloat16, as the task asks"):
            nc.vector.tensor_reduce(state[:, LAST_START:], half_sums[:], INNERMOST, ADD)

        stationary = []
        for blocks_in_store in BLOCKS_IN_STORE:
            first_word = len(stationary) * BLOCK
            blocks = weights[:, first_word : first_word + blocks_in_store * BLOCK].rearrange("c (p j) -> c j p", p=BLOCK)
            for j in range(blocks_in_store):
                stationary.append(blocks[:, j, :])
        early_products = []
        for k in range(EARLY_BLOCKS):
            product = banks.tile([BLOCK, B], F32, name="product")
            nc.tensor.matmul(
                product[:, :SCALAR_QUESTIONS], stationary[k], state[:, :SCALAR_QUESTIONS], start=True, stop=True
            )
            early_products.append(product)
        first_block = 0
        for blocks_in_store in BLOCKS_IN_STORE:
            staged = staging.tile([BLOCK, blocks_in_store, B], F32, name=f"staged{blocks_in_store}")
            for j in range(blocks_in_store):
                k = first_block + j
                if k < EARLY_BLOCKS:
                    product = early_products[k]
                    first_column = SCALAR_QUESTIONS
                else:
                    product = banks.tile([BLOCK, B], F32, name="product")
                    first_column = 0
                nc.tensor.matmul(
                    product[:, first_column:], stationary[k], state[:, first_column:], start=True, stop=True
                )
                if j % 2 == 0:
                    nc.vector.tensor_copy(staged[:, j, :], product[:])
                else:
                    nc.scalar.activation(staged[:, j, :], product[:], COPY)
            first_word = first_block * BLOCK
            nc.sync.dma_start(
                out[first_word : first_word + blocks_in_store * BLOCK, :].rearrange("(p j) b -> p j b", p=BLOCK),
                staged[:],
            )
            first_block += blocks_in_store
